import numpy as np
import ml_dtypes


def mxq(x, axis, fmt="e4m3"):
    dtype, down = {"e4m3": (ml_dtypes.float8_e4m3fn, 7), "e5m2": (ml_dtypes.float8_e5m2, 14)}[fmt]
    v = np.moveaxis(np.asarray(x, np.float32).astype(ml_dtypes.bfloat16).astype(np.float64), axis, -1)
    blocks = v.reshape(v.shape[:-1] + (-1, 32))
    amax = np.abs(blocks).max(-1, keepdims=True)
    byte = np.maximum(np.where(amax > 0, np.frexp(amax)[1] - 1 + 127, 0) - down, 1)
    scale = np.exp2(byte - 127.0)
    codes = (blocks / scale).astype(np.float32).astype(dtype).astype(np.float64)
    return np.moveaxis((codes * scale).reshape(v.shape), -1, axis)


WIDE = False


def mx_kscale(k):
    if not WIDE:
        return np.ones(k)
    levels = np.array([10, -10, 5, -5, 0])
    a = np.random.permutation(np.resize(levels, k // 512 * 4)).reshape(k // 512, 4)
    idx = np.arange(k)
    return np.exp2(a[idx // 512, idx % 128 // 32])


BF16 = ml_dtypes.bfloat16


def bf(x):
    return np.asarray(x, np.float32).astype(BF16)


def f64(x):
    return np.asarray(x).astype(np.float64)


E2M1 = np.array([0.0, 0.5, 1.0, 1.5, 2.0, 3.0, 4.0, 6.0, -0.0, -0.5, -1.0, -1.5, -2.0, -3.0, -4.0, -6.0])


def pack_weight(w, fmt):
    k, n = w.shape
    w = f64(bf(w)).reshape(k // 32, 32, n)
    amax = np.abs(w).max(1)
    if fmt == "e4m3":
        byte = np.frexp(amax)[1] - 1 + 127 - 7
    else:
        mant, ex = np.frexp(amax / 6.0)
        byte = np.where(mant > 0.5, ex, ex - 1) + 127
    byte = np.clip(np.where(amax > 0, byte, 1), 1, 254)
    scaled = (w * np.exp2(127.0 - byte)[:, None, :]).reshape(k, n).astype(np.float32)
    by_word = np.ascontiguousarray(scaled.reshape(k // 512, 128, 4, n).transpose(0, 1, 3, 2))
    if fmt == "e4m3":
        words = by_word.astype(ml_dtypes.float8_e4m3fn).view(np.uint8)
    else:
        c = by_word.astype(ml_dtypes.float4_e2m1fn).view(np.uint8) & 0xF
        words = c[..., 0::2] | (c[..., 1::2] << 4)
    return np.ascontiguousarray(words), np.ascontiguousarray(byte.astype(np.uint8).reshape(k // 512, 16, n))


def unpack_weight(words, scales, fmt):
    g, p, n, _ = words.shape
    if fmt == "e4m3":
        vals = np.ascontiguousarray(words).view(ml_dtypes.float8_e4m3fn).astype(np.float64)
    else:
        nib = np.empty((g, p, n, 4), np.uint8)
        nib[..., 0::2] = words & 0xF
        nib[..., 1::2] = words >> 4
        vals = E2M1[nib]
    vals = vals * np.repeat(np.exp2(scales.astype(np.float64) - 127.0), 8, axis=1)[..., None]
    return vals.transpose(0, 1, 3, 2).reshape(g * 512, n)


B, C, PS, G, E = 24, 3, 64, 4, 512
NP = G * G
M1 = NP // 2
K2 = 2 * E
FMT = "e4m3"


def setup_inputs():
    t = mx_kscale(K2)[:E]
    tt = np.concatenate([t, t])
    h1 = bf(np.random.standard_normal((B, NP, M1, E)) * t)
    cross_w = np.random.standard_normal((E, K2)) / np.sqrt(K2) * t[:, None] / tt[None, :]
    words, scales = pack_weight(np.ascontiguousarray(cross_w.T), FMT)
    cross_b = bf(np.random.standard_normal(E) * 0.3 * t)
    return {"h1": h1,
            "cross_w_words": words,
            "cross_w_scales": scales,
            "cross_b": cross_b}


def reference(h1, cross_w_words, cross_w_scales, cross_b):
    wt = unpack_weight(cross_w_words, cross_w_scales, FMT)
    bias = f64(cross_b)
    g1 = f64(h1).reshape(B, NP, M1 // 2, K2)
    h2 = (mxq(g1, 3, "e4m3") @ wt) + bias
    g2 = h2.reshape(B, NP, M1 // 4, K2)
    return (mxq(g2, 3, "e4m3") @ wt) + bias

@@ -1,0 +1,185 @@
+from contextlib import ExitStack
+
+import concourse.mybir as mybir
+from concourse.masks import make_identity
+
+BF16 = mybir.dt.bfloat16
+F32 = mybir.dt.float32
+I32 = mybir.dt.int32
+U32 = mybir.dt.uint32
+U8 = mybir.dt.uint8
+FP8X4 = mybir.dt.float8_e4m3fn_x4
+
+P = 128
+PACK = 4
+K_PASS = P * PACK
+E = 512
+K2 = 2 * E
+PASSES = K2 // K_PASS
+SIDES = 2
+HALVES = 2
+ROWS_OUT = 24 * 16 * 2
+N_TILES = ROWS_OUT // P
+SCALE_ROWS = 4
+QUADRANT = 32
+
+FLOPS = 2 * (SIDES * ROWS_OUT) * K2 * E + 2 * ROWS_OUT * K2 * E
+
+WORK_BUFS = 2 * SIDES
+
+
+def tile_simplemodel_pc_kernel(tc, h1, cross_w_words, cross_w_scales, cross_b, out):
+    nc = tc.nc
+    x_rows = h1.flatten_outer_dims().rearrange("(r c) k -> r (c k)", c=SIDES * 2)
+    out_rows = out.flatten_outer_dims()
+
+    with ExitStack() as stack:
+        keep = stack.enter_context(tc.tile_pool(name="keep", bufs=1))
+        work = stack.enter_context(tc.tile_pool(name="work", bufs=WORK_BUFS))
+        psum = stack.enter_context(tc.psum_pool(name="psum", bufs=SIDES))
+        stack.enter_context(tc.manual_schedule())
+
+        w_scales = keep.tile([P, PASSES, E], U8, align_bytes=64)
+        nc.vector.memset(w_scales[:].bitcast(I32), 0)
+        bias_rows = keep.tile([P, E], BF16)
+        nc.vector.memset(bias_rows[:], 0.0)
+        ones = keep.tile([P, P], BF16)
+        nc.vector.memset(ones[:], 1.0)
+        ident_f32 = keep.tile([P, P], F32)
+        make_identity(nc, ident_f32[:])
+        ident_bf16 = keep.tile([P, P], BF16)
+        make_identity(nc, ident_bf16[:])
+
+        nc.scalar.dma_start(out=bias_rows[0:1, :], in_=cross_b.unsqueeze(0))
+
+        x_sb = {}
+
+        def load_x(i):
+            for s in range(SIDES):
+                x_sb[(i, s)] = keep.tile([P, K2], BF16, name="x_%d_%d" % (i, s))
+                nc.sync.dma_start(
+                    out=x_sb[(i, s)][:],
+                    in_=x_rows[i * P : (i + 1) * P, s * K2 : (s + 1) * K2],
+                )
+
+        load_x(0)
+        scale_words = cross_w_scales.bitcast(I32).rearrange("g (a r) n -> r a g n", r=SCALE_ROWS)
+        for r in range(SCALE_ROWS):
+            nc.sync.dma_start(out=w_scales[r:P:QUADRANT, :, :].bitcast(I32), in_=scale_words[r])
+        w_words = keep.tile([P, PASSES, E * PACK], U8, align_bytes=64)
+        for g in range(PASSES):
+            nc.sync.dma_start(
+                out=w_words[:, g, :].bitcast(I32),
+                in_=cross_w_words[g].rearrange("p n t -> p (n t)").bitcast(I32),
+            )
+        for i in range(1, N_TILES):
+            load_x(i)
+
+        bias_plain = keep.tile([P, E], F32)
+        bias_by_code = keep.tile([P, PACK, P], F32)
+
+        def spread_bias():
+            bias_ps = psum.tile([P, E], F32, name="out_ps")
+            nc.tensor.matmul(out=bias_ps[:], lhsT=ones[:], rhs=bias_rows[:], start=True, stop=True)
+            nc.vector.tensor_copy(
+                out=bias_by_code[:], in_=bias_ps[:].rearrange("p (q t) -> p t q", t=PACK)
+            )
+            nc.vector.tensor_copy(out=bias_plain[:], in_=bias_ps[:])
+
+        g1_codes, g1_scales, h2_sb, g2_grouped, g2_codes, g2_scales = {}, {}, {}, {}, {}, {}
+
+        def quantise_g1(i):
+            for s in range(SIDES):
+                x_words = x_sb[(i, s)][:].bitcast(F32)
+                xT = psum.tile([P, PASSES, HALVES, P], F32, name="xT")
+                for g in range(PASSES):
+                    for u in range(HALVES):
+                        first = g * (K_PASS // 2) + u
+                        nc.tensor.transpose(
+                            xT[:, g, u, :],
+                            x_words[:, first : (g + 1) * (K_PASS // 2) : HALVES],
+                            ident_f32[:],
+                        )
+                grouped = work.tile([P, PASSES, P, PACK], BF16, name="g1_grouped", align_bytes=64)
+                nc.scalar.copy(out=grouped[:].bitcast(F32), in_=xT[:].rearrange("p g u c -> p g c u"))
+                g1_codes[(i, s)] = work.tile([P, PASSES, P], U32, name="g1_codes", align_bytes=64)
+                g1_scales[(i, s)] = work.tile([P, PASSES, P], U8, name="g1_scales", align_bytes=64)
+                nc.vector.quantize_mx(
+                    out=g1_codes[(i, s)][:].rearrange("p g c -> p (g c)").bitcast(FP8X4),
+                    scales=g1_scales[(i, s)][:].rearrange("p g c -> p (g c)"),
+                    in_=grouped[:].rearrange("p g c t -> p (g c t)"),
+                )
+
+        def level_one(i):
+            for s in range(SIDES):
+                h2_ps = psum.tile([P, E], F32, name="h2_ps")
+                for g in range(PASSES):
+                    nc.tensor.matmul_mx(
+                        out=h2_ps[:],
+                        lhsT=g1_codes[(i, s)][:, g, :].bitcast(FP8X4),
+                        lhsT_scale=g1_scales[(i, s)][:, g, :],
+                        rhs=w_words[:, g, :].bitcast(FP8X4),
+                        rhs_scale=w_scales[:, g, :],
+                        start=(g == 0),
+                        stop=(g == PASSES - 1),
+                    )
+                h2_sb[(i, s)] = work.tile([P, PACK, P], BF16, name="h2_sb")
+                nc.vector.tensor_tensor(
+                    out=h2_sb[(i, s)][:],
+                    in0=h2_ps[:].rearrange("p (q t) -> p t q", t=PACK),
+                    in1=bias_by_code[:],
+                    op=mybir.AluOpType.add,
+                )
+
+        def transpose_h2(i):
+            for s in range(SIDES):
+                hT = psum.tile([P, PACK, P], BF16, name="hT")
+                for t in range(PACK):
+                    nc.tensor.transpose(hT[:, t, :], h2_sb[(i, s)][:, t, :], ident_bf16[:])
+                g2_grouped[(i, s)] = work.tile([P, P, PACK], BF16, name="g2_grouped", align_bytes=64)
+                nc.scalar.copy(out=g2_grouped[(i, s)][:], in_=hT[:].rearrange("p t c -> p c t"))
+
+        def quantise_g2(i):
+            for s in range(SIDES):
+                g2_codes[(i, s)] = work.tile([P, P], U32, name="g2_codes", align_bytes=64)
+                g2_scales[(i, s)] = work.tile([P, P], U8, name="g2_scales", align_bytes=64)
+                nc.vector.quantize_mx(
+                    out=g2_codes[(i, s)][:].bitcast(FP8X4),
+                    scales=g2_scales[(i, s)][:],
+                    in_=g2_grouped[(i, s)][:].rearrange("p c t -> p (c t)"),
+                )
+
+        def level_two(i):
+            out_ps = psum.tile([P, E], F32, name="out_ps")
+            for s in range(SIDES):
+                nc.tensor.matmul_mx(
+                    out=out_ps[:],
+                    lhsT=g2_codes[(i, s)][:].bitcast(FP8X4),
+                    lhsT_scale=g2_scales[(i, s)][:],
+                    rhs=w_words[:, s, :].bitcast(FP8X4),
+                    rhs_scale=w_scales[:, s, :],
+                    start=(s == 0),
+                    stop=(s == SIDES - 1),
+                )
+            out_sb = work.tile([P, E], F32, name="out_sb")
+            nc.vector.tensor_tensor(
+                out=out_sb[:], in0=out_ps[:], in1=bias_plain[:], op=mybir.AluOpType.add
+            )
+            nc.sync.dma_start(out=out_rows[i * P : (i + 1) * P, :], in_=out_sb[:])
+
+        def in_range(i):
+            return 0 <= i < N_TILES
+
+        quantise_g1(0)
+        spread_bias()
+        for j in range(1, N_TILES + 3):
+            if in_range(j):
+                quantise_g1(j)
+            if in_range(j - 2):
+                transpose_h2(j - 2)
+            if in_range(j - 1):
+                level_one(j - 1)
+            if in_range(j - 2):
+                quantise_g2(j - 2)
+            if in_range(j - 3):
+                level_two(j - 3)

@@ -26,6 +26,7 @@ QUADRANT = 32
 FLOPS = 2 * (SIDES * ROWS_OUT) * K2 * E + 2 * ROWS_OUT * K2 * E
 
 WORK_BUFS = 2 * SIDES
+TILES_BEFORE_W = 2
 
 
 def tile_simplemodel_pc_kernel(tc, h1, cross_w_words, cross_w_scales, cross_b, out):
@@ -62,7 +63,8 @@ def tile_simplemodel_pc_kernel(tc, h1, cross_w_words, cross_w_scales, cross_b, o
                     in_=x_rows[i * P : (i + 1) * P, s * K2 : (s + 1) * K2],
                 )
 
-        load_x(0)
+        for i in range(TILES_BEFORE_W):
+            load_x(i)
         scale_words = cross_w_scales.bitcast(I32).rearrange("g (a r) n -> r a g n", r=SCALE_ROWS)
         for r in range(SCALE_ROWS):
             nc.sync.dma_start(out=w_scales[r:P:QUADRANT, :, :].bitcast(I32), in_=scale_words[r])
@@ -72,7 +74,7 @@ def tile_simplemodel_pc_kernel(tc, h1, cross_w_words, cross_w_scales, cross_b, o
                 out=w_words[:, g, :].bitcast(I32),
                 in_=cross_w_words[g].rearrange("p n t -> p (n t)").bitcast(I32),
             )
-        for i in range(1, N_TILES):
+        for i in range(TILES_BEFORE_W, N_TILES):
             load_x(i)
 
         bias_plain = keep.tile([P, E], F32)

@@ -27,6 +27,7 @@ FLOPS = 2 * (SIDES * ROWS_OUT) * K2 * E + 2 * ROWS_OUT * K2 * E
 
 WORK_BUFS = 2 * SIDES
 TILES_BEFORE_W = 2
+WARM_UP_MATMULS = 5
 
 
 def tile_simplemodel_pc_kernel(tc, h1, cross_w_words, cross_w_scales, cross_b, out):
@@ -40,12 +41,14 @@ def tile_simplemodel_pc_kernel(tc, h1, cross_w_words, cross_w_scales, cross_b, o
         psum = stack.enter_context(tc.psum_pool(name="psum", bufs=SIDES))
         stack.enter_context(tc.manual_schedule())
 
-        w_scales = keep.tile([P, PASSES, E], U8, align_bytes=64)
-        nc.vector.memset(w_scales[:].bitcast(I32), 0)
-        bias_rows = keep.tile([P, E], BF16)
-        nc.vector.memset(bias_rows[:], 0.0)
         ones = keep.tile([P, P], BF16)
         nc.vector.memset(ones[:], 1.0)
+        zeros = keep.tile([P, E], BF16)
+        nc.vector.memset(zeros[:], 0.0)
+        bias_rows = keep.tile([P, E], BF16)
+        nc.vector.memset(bias_rows[:], 0.0)
+        w_scales = keep.tile([P, PASSES, E], U8, align_bytes=64)
+        nc.vector.memset(w_scales[:].bitcast(I32), 0)
         ident_f32 = keep.tile([P, P], F32)
         make_identity(nc, ident_f32[:])
         ident_bf16 = keep.tile([P, P], BF16)
@@ -76,6 +79,17 @@ def tile_simplemodel_pc_kernel(tc, h1, cross_w_words, cross_w_scales, cross_b, o
             )
         for i in range(TILES_BEFORE_W, N_TILES):
             load_x(i)
+
+        def warm_up():
+            unread = psum.tile([P, E], F32, name="h2_ps")
+            for n in range(WARM_UP_MATMULS):
+                nc.tensor.matmul(
+                    out=unread[:],
+                    lhsT=ones[:],
+                    rhs=zeros[:],
+                    start=(n == 0),
+                    stop=(n == WARM_UP_MATMULS - 1),
+                )
 
         bias_plain = keep.tile([P, E], F32)
         bias_by_code = keep.tile([P, PACK, P], F32)
@@ -172,6 +186,7 @@ def tile_simplemodel_pc_kernel(tc, h1, cross_w_words, cross_w_scales, cross_b, o
         def in_range(i):
             return 0 <= i < N_TILES
 
+        warm_up()
         quantise_g1(0)
         spread_bias()
         for j in range(1, N_TILES + 3):

@@ -26,7 +26,9 @@ QUADRANT = 32
 FLOPS = 2 * (SIDES * ROWS_OUT) * K2 * E + 2 * ROWS_OUT * K2 * E
 
 WORK_BUFS = 2 * SIDES
-TILES_BEFORE_W = 2
+XT_BANKS = 3
+H2_BANKS = 3
+OUT_BANKS = 2
 WARM_UP_MATMULS = 5
 
 
@@ -38,36 +40,24 @@ def tile_simplemodel_pc_kernel(tc, h1, cross_w_words, cross_w_scales, cross_b, o
     with ExitStack() as stack:
         keep = stack.enter_context(tc.tile_pool(name="keep", bufs=1))
         work = stack.enter_context(tc.tile_pool(name="work", bufs=WORK_BUFS))
-        psum = stack.enter_context(tc.psum_pool(name="psum", bufs=SIDES))
+        psum = stack.enter_context(tc.psum_pool(name="psum", bufs=OUT_BANKS))
         stack.enter_context(tc.manual_schedule())
 
+        w_scales = keep.tile([P, PASSES, E], U8, align_bytes=64)
+        nc.gpsimd.memset(w_scales[:].bitcast(F32), 0.0)
+        bias_rows = keep.tile([P, E], BF16)
+        nc.vector.memset(bias_rows[:], 0.0)
         ones = keep.tile([P, P], BF16)
         nc.vector.memset(ones[:], 1.0)
         zeros = keep.tile([P, E], BF16)
         nc.vector.memset(zeros[:], 0.0)
-        bias_rows = keep.tile([P, E], BF16)
-        nc.vector.memset(bias_rows[:], 0.0)
-        w_scales = keep.tile([P, PASSES, E], U8, align_bytes=64)
-        nc.vector.memset(w_scales[:].bitcast(I32), 0)
         ident_f32 = keep.tile([P, P], F32)
         make_identity(nc, ident_f32[:])
-        ident_bf16 = keep.tile([P, P], BF16)
-        make_identity(nc, ident_bf16[:])
 
         nc.scalar.dma_start(out=bias_rows[0:1, :], in_=cross_b.unsqueeze(0))
+        bias_by_code = keep.tile([P, PACK], BF16)
+        nc.scalar.dma_start(out=bias_by_code[:], in_=cross_b.rearrange("(p t) -> p t", t=PACK))
 
-        x_sb = {}
-
-        def load_x(i):
-            for s in range(SIDES):
-                x_sb[(i, s)] = keep.tile([P, K2], BF16, name="x_%d_%d" % (i, s))
-                nc.sync.dma_start(
-                    out=x_sb[(i, s)][:],
-                    in_=x_rows[i * P : (i + 1) * P, s * K2 : (s + 1) * K2],
-                )
-
-        for i in range(TILES_BEFORE_W):
-            load_x(i)
         scale_words = cross_w_scales.bitcast(I32).rearrange("g (a r) n -> r a g n", r=SCALE_ROWS)
         for r in range(SCALE_ROWS):
             nc.sync.dma_start(out=w_scales[r:P:QUADRANT, :, :].bitcast(I32), in_=scale_words[r])
@@ -77,11 +67,29 @@ def tile_simplemodel_pc_kernel(tc, h1, cross_w_words, cross_w_scales, cross_b, o
                 out=w_words[:, g, :].bitcast(I32),
                 in_=cross_w_words[g].rearrange("p n t -> p (n t)").bitcast(I32),
             )
-        for i in range(TILES_BEFORE_W, N_TILES):
-            load_x(i)
+        x_sb = {}
+        for i in range(N_TILES):
+            for s in range(SIDES):
+                x_sb[(i, s)] = keep.tile([P, K2], BF16, name="x_%d_%d" % (i, s))
+                nc.sync.dma_start(
+                    out=x_sb[(i, s)][:],
+                    in_=x_rows[i * P : (i + 1) * P, s * K2 : (s + 1) * K2],
+                )
+
+        w_scales_sorted = keep.tile([P, PASSES, PACK, P], U8, align_bytes=64)
+        nc.vector.tensor_copy(
+            out=w_scales_sorted[:].rearrange("p g t m -> p g m t"),
+            in_=w_scales[:].rearrange("p g (m t) -> p g m t", t=PACK),
+        )
+        w_words_sorted = keep.tile([P, PASSES, PACK, P], I32, align_bytes=64)
+        for g in range(PASSES):
+            nc.vector.tensor_copy(
+                out=w_words_sorted[:, g, :, :],
+                in_=w_words[:, g, :].bitcast(I32).rearrange("p (m t) -> p t m", t=PACK),
+            )
 
         def warm_up():
-            unread = psum.tile([P, E], F32, name="h2_ps")
+            unread = psum.tile([P, E], F32, name="h2T", bufs=H2_BANKS)
             for n in range(WARM_UP_MATMULS):
                 nc.tensor.matmul(
                     out=unread[:],
@@ -92,22 +100,18 @@ def tile_simplemodel_pc_kernel(tc, h1, cross_w_words, cross_w_scales, cross_b, o
                 )
 
         bias_plain = keep.tile([P, E], F32)
-        bias_by_code = keep.tile([P, PACK, P], F32)
 
         def spread_bias():
             bias_ps = psum.tile([P, E], F32, name="out_ps")
             nc.tensor.matmul(out=bias_ps[:], lhsT=ones[:], rhs=bias_rows[:], start=True, stop=True)
-            nc.vector.tensor_copy(
-                out=bias_by_code[:], in_=bias_ps[:].rearrange("p (q t) -> p t q", t=PACK)
-            )
             nc.vector.tensor_copy(out=bias_plain[:], in_=bias_ps[:])
 
-        g1_codes, g1_scales, h2_sb, g2_grouped, g2_codes, g2_scales = {}, {}, {}, {}, {}, {}
+        g1_codes, g1_scales, g2_grouped, g2_codes, g2_scales = {}, {}, {}, {}, {}
 
         def quantise_g1(i):
             for s in range(SIDES):
                 x_words = x_sb[(i, s)][:].bitcast(F32)
-                xT = psum.tile([P, PASSES, HALVES, P], F32, name="xT")
+                xT = psum.tile([P, PASSES, HALVES, P], F32, name="xT", bufs=XT_BANKS)
                 for g in range(PASSES):
                     for u in range(HALVES):
                         first = g * (K_PASS // 2) + u
@@ -128,32 +132,25 @@ def tile_simplemodel_pc_kernel(tc, h1, cross_w_words, cross_w_scales, cross_b, o
 
         def level_one(i):
             for s in range(SIDES):
-                h2_ps = psum.tile([P, E], F32, name="h2_ps")
-                for g in range(PASSES):
-                    nc.tensor.matmul_mx(
-                        out=h2_ps[:],
-                        lhsT=g1_codes[(i, s)][:, g, :].bitcast(FP8X4),
-                        lhsT_scale=g1_scales[(i, s)][:, g, :],
-                        rhs=w_words[:, g, :].bitcast(FP8X4),
-                        rhs_scale=w_scales[:, g, :],
-                        start=(g == 0),
-                        stop=(g == PASSES - 1),
-                    )
-                h2_sb[(i, s)] = work.tile([P, PACK, P], BF16, name="h2_sb")
+                h2T = psum.tile([P, PACK, P], F32, name="h2T", bufs=H2_BANKS)
+                for t in range(PACK):
+                    for g in range(PASSES):
+                        nc.tensor.matmul_mx(
+                            out=h2T[:, t, :],
+                            lhsT=w_words_sorted[:, g, t, :].bitcast(FP8X4),
+                            lhsT_scale=w_scales_sorted[:, g, t, :],
+                            rhs=g1_codes[(i, s)][:, g, :].bitcast(FP8X4),
+                            rhs_scale=g1_scales[(i, s)][:, g, :],
+                            start=(g == 0),
+                            stop=(g == PASSES - 1),
+                        )
+                g2_grouped[(i, s)] = work.tile([P, P, PACK], BF16, name="g2_grouped", align_bytes=64)
                 nc.vector.tensor_tensor(
-                    out=h2_sb[(i, s)][:],
-                    in0=h2_ps[:].rearrange("p (q t) -> p t q", t=PACK),
-                    in1=bias_by_code[:],
+                    out=g2_grouped[(i, s)][:],
+                    in0=h2T[:].rearrange("p t c -> p c t"),
+                    in1=bias_by_code[:].unsqueeze(1).to_broadcast([P, P, PACK]),
                     op=mybir.AluOpType.add,
                 )
-
-        def transpose_h2(i):
-            for s in range(SIDES):
-                hT = psum.tile([P, PACK, P], BF16, name="hT")
-                for t in range(PACK):
-                    nc.tensor.transpose(hT[:, t, :], h2_sb[(i, s)][:, t, :], ident_bf16[:])
-                g2_grouped[(i, s)] = work.tile([P, P, PACK], BF16, name="g2_grouped", align_bytes=64)
-                nc.scalar.copy(out=g2_grouped[(i, s)][:], in_=hT[:].rearrange("p t c -> p c t"))
 
         def quantise_g2(i):
             for s in range(SIDES):
@@ -187,16 +184,12 @@ def tile_simplemodel_pc_kernel(tc, h1, cross_w_words, cross_w_scales, cross_b, o
             return 0 <= i < N_TILES
 
         warm_up()
-        quantise_g1(0)
         spread_bias()
-        for j in range(1, N_TILES + 3):
+        for j in range(N_TILES + 2):
             if in_range(j):
                 quantise_g1(j)
-            if in_range(j - 2):
-                transpose_h2(j - 2)
             if in_range(j - 1):
                 level_one(j - 1)
+                quantise_g2(j - 1)
             if in_range(j - 2):
-                quantise_g2(j - 2)
-            if in_range(j - 3):
-                level_two(j - 3)
+                level_two(j - 2)

@@ -29,6 +29,15 @@ WORK_BUFS = 2 * SIDES
 XT_BANKS = 3
 H2_BANKS = 3
 OUT_BANKS = 2
+SORT_FROM_TILE = 6
+TILES_BEFORE_W = 0
+LEAD_T = 1
+LAG_L2 = 1
+SCALAR_B = ()
+MERGE_Q1 = False
+MERGE_Q2 = False
+V_ORDER = 0
+LAST_PIECES = 2
 WARM_UP_MATMULS = 5
 
 
@@ -58,17 +67,9 @@ def tile_simplemodel_pc_kernel(tc, h1, cross_w_words, cross_w_scales, cross_b, o
         bias_by_code = keep.tile([P, PACK], BF16)
         nc.scalar.dma_start(out=bias_by_code[:], in_=cross_b.rearrange("(p t) -> p t", t=PACK))
 
-        scale_words = cross_w_scales.bitcast(I32).rearrange("g (a r) n -> r a g n", r=SCALE_ROWS)
-        for r in range(SCALE_ROWS):
-            nc.sync.dma_start(out=w_scales[r:P:QUADRANT, :, :].bitcast(I32), in_=scale_words[r])
-        w_words = keep.tile([P, PASSES, E * PACK], U8, align_bytes=64)
-        for g in range(PASSES):
-            nc.sync.dma_start(
-                out=w_words[:, g, :].bitcast(I32),
-                in_=cross_w_words[g].rearrange("p n t -> p (n t)").bitcast(I32),
-            )
         x_sb = {}
-        for i in range(N_TILES):
+
+        def load_x(i):
             for s in range(SIDES):
                 x_sb[(i, s)] = keep.tile([P, K2], BF16, name="x_%d_%d" % (i, s))
                 nc.sync.dma_start(
@@ -76,27 +77,42 @@ def tile_simplemodel_pc_kernel(tc, h1, cross_w_words, cross_w_scales, cross_b, o
                     in_=x_rows[i * P : (i + 1) * P, s * K2 : (s + 1) * K2],
                 )
 
-        w_scales_sorted = keep.tile([P, PASSES, PACK, P], U8, align_bytes=64)
-        nc.vector.tensor_copy(
-            out=w_scales_sorted[:].rearrange("p g t m -> p g m t"),
-            in_=w_scales[:].rearrange("p g (m t) -> p g m t", t=PACK),
-        )
-        w_words_sorted = keep.tile([P, PASSES, PACK, P], I32, align_bytes=64)
+        scale_words = cross_w_scales.bitcast(I32).rearrange("g (a r) n -> r a g n", r=SCALE_ROWS)
+        for r in range(SCALE_ROWS):
+            nc.sync.dma_start(out=w_scales[r:P:QUADRANT, :, :].bitcast(I32), in_=scale_words[r])
+        for i in range(TILES_BEFORE_W):
+            load_x(i)
+        w_words = keep.tile([P, PASSES, E * PACK], U8, align_bytes=64)
         for g in range(PASSES):
-            nc.vector.tensor_copy(
-                out=w_words_sorted[:, g, :, :],
-                in_=w_words[:, g, :].bitcast(I32).rearrange("p (m t) -> p t m", t=PACK),
+            nc.sync.dma_start(
+                out=w_words[:, g, :].bitcast(I32),
+                in_=cross_w_words[g].rearrange("p n t -> p (n t)").bitcast(I32),
             )
+        for i in range(TILES_BEFORE_W, N_TILES):
+            load_x(i)
+
+        w_scales_sorted = keep.tile([P, PASSES, PACK, P], U8, align_bytes=64)
+        w_words_sorted = keep.tile([P, PASSES, PACK, P], I32, align_bytes=64)
+
+        def sort_w_scales():
+            nc.vector.tensor_copy(
+                out=w_scales_sorted[:].rearrange("p g t m -> p g m t"),
+                in_=w_scales[:].rearrange("p g (m t) -> p g m t", t=PACK),
+            )
+
+        def sort_w_words():
+            for g in range(PASSES):
+                nc.vector.tensor_copy(
+                    out=w_words_sorted[:, g, :, :],
+                    in_=w_words[:, g, :].bitcast(I32).rearrange("p (m t) -> p t m", t=PACK),
+                )
 
         def warm_up():
             unread = psum.tile([P, E], F32, name="h2T", bufs=H2_BANKS)
             for n in range(WARM_UP_MATMULS):
                 nc.tensor.matmul(
-                    out=unread[:],
-                    lhsT=ones[:],
-                    rhs=zeros[:],
-                    start=(n == 0),
-                    stop=(n == WARM_UP_MATMULS - 1),
+                    out=unread[:], lhsT=ones[:], rhs=zeros[:],
+                    start=(n == 0), stop=(n == WARM_UP_MATMULS - 1),
                 )
 
         bias_plain = keep.tile([P, E], F32)
@@ -104,92 +120,177 @@ def tile_simplemodel_pc_kernel(tc, h1, cross_w_words, cross_w_scales, cross_b, o
         def spread_bias():
             bias_ps = psum.tile([P, E], F32, name="out_ps")
             nc.tensor.matmul(out=bias_ps[:], lhsT=ones[:], rhs=bias_rows[:], start=True, stop=True)
-            nc.vector.tensor_copy(out=bias_plain[:], in_=bias_ps[:])
+            nc.scalar.copy(out=bias_plain[:], in_=bias_ps[:])
 
-        g1_codes, g1_scales, g2_grouped, g2_codes, g2_scales = {}, {}, {}, {}, {}
+        x_sorted, xT, g1_grouped, g1_codes, g1_scales = {}, {}, {}, {}, {}
+        h2T, g2_grouped, g2_codes, g2_scales = {}, {}, {}, {}
 
-        def quantise_g1(i):
-            for s in range(SIDES):
-                x_words = x_sb[(i, s)][:].bitcast(F32)
-                xT = psum.tile([P, PASSES, HALVES, P], F32, name="xT", bufs=XT_BANKS)
+        def sort_words(i, s):
+            x_sorted[(i, s)] = work.tile([P, PASSES, HALVES, P], F32, name="x_sorted")
+            nc.scalar.copy(
+                out=x_sorted[(i, s)][:],
+                in_=x_sb[(i, s)][:].bitcast(F32).rearrange("p (g q u) -> p g u q", g=PASSES, u=HALVES),
+            )
+
+        def transposes(i, s):
+            x_words = x_sb[(i, s)][:].bitcast(F32)
+            xT[(i, s)] = psum.tile([P, PASSES, HALVES, P], F32, name="xT", bufs=XT_BANKS)
+            for g in range(PASSES):
+                for u in range(HALVES):
+                    first = g * (K_PASS // 2) + u
+                    nc.tensor.transpose(
+                        xT[(i, s)][:, g, u, :],
+                        x_sorted[(i, s)][:, g, u, :]
+                        if i >= SORT_FROM_TILE
+                        else x_words[:, first : (g + 1) * (K_PASS // 2) : HALVES],
+                        ident_f32[:],
+                    )
+
+        def new_g1(i):
+            g1_grouped[i] = work.tile([P, SIDES, PASSES, P, PACK], BF16, name="g1_grouped", bufs=SIDES, align_bytes=64)
+            g1_codes[i] = work.tile([P, SIDES, PASSES, P], U32, name="g1_codes", bufs=3, align_bytes=64)
+            g1_scales[i] = work.tile([P, SIDES, PASSES, P], U8, name="g1_scales", bufs=3, align_bytes=64)
+
+        def evacuate_x(i, s):
+            nc.scalar.copy(
+                out=g1_grouped[i][:, s].bitcast(F32), in_=xT[(i, s)][:].rearrange("p g u c -> p g c u")
+            )
+
+        def quantise_g1(i, sides):
+            lo, hi = sides[0], sides[-1] + 1
+            nc.vector.quantize_mx(
+                out=g1_codes[i][:, lo:hi].rearrange("p s g c -> p (s g c)").bitcast(FP8X4),
+                scales=g1_scales[i][:, lo:hi].rearrange("p s g c -> p (s g c)"),
+                in_=g1_grouped[i][:, lo:hi].rearrange("p s g c t -> p (s g c t)"),
+            )
+
+        def level_one(i, s):
+            h2T[(i, s)] = psum.tile([P, PACK, P], F32, name="h2T", bufs=H2_BANKS)
+            for t in range(PACK):
                 for g in range(PASSES):
-                    for u in range(HALVES):
-                        first = g * (K_PASS // 2) + u
-                        nc.tensor.transpose(
-                            xT[:, g, u, :],
-                            x_words[:, first : (g + 1) * (K_PASS // 2) : HALVES],
-                            ident_f32[:],
-                        )
-                grouped = work.tile([P, PASSES, P, PACK], BF16, name="g1_grouped", align_bytes=64)
-                nc.scalar.copy(out=grouped[:].bitcast(F32), in_=xT[:].rearrange("p g u c -> p g c u"))
-                g1_codes[(i, s)] = work.tile([P, PASSES, P], U32, name="g1_codes", align_bytes=64)
-                g1_scales[(i, s)] = work.tile([P, PASSES, P], U8, name="g1_scales", align_bytes=64)
-                nc.vector.quantize_mx(
-                    out=g1_codes[(i, s)][:].rearrange("p g c -> p (g c)").bitcast(FP8X4),
-                    scales=g1_scales[(i, s)][:].rearrange("p g c -> p (g c)"),
-                    in_=grouped[:].rearrange("p g c t -> p (g c t)"),
-                )
+                    nc.tensor.matmul_mx(
+                        out=h2T[(i, s)][:, t, :],
+                        lhsT=w_words_sorted[:, g, t, :].bitcast(FP8X4),
+                        lhsT_scale=w_scales_sorted[:, g, t, :],
+                        rhs=g1_codes[i][:, s, g, :].bitcast(FP8X4),
+                        rhs_scale=g1_scales[i][:, s, g, :],
+                        start=(g == 0),
+                        stop=(g == PASSES - 1),
+                    )
 
-        def level_one(i):
-            for s in range(SIDES):
-                h2T = psum.tile([P, PACK, P], F32, name="h2T", bufs=H2_BANKS)
+        def new_g2(i):
+            g2_grouped[i] = work.tile([P, SIDES, P, PACK], BF16, name="g2_grouped", bufs=3, align_bytes=64)
+            g2_codes[i] = work.tile([P, SIDES, P], U32, name="g2_codes", bufs=3, align_bytes=64)
+            g2_scales[i] = work.tile([P, SIDES, P], U8, name="g2_scales", bufs=3, align_bytes=64)
+
+        def add_bias(i, s):
+            if (i, s) in SCALAR_B:
                 for t in range(PACK):
-                    for g in range(PASSES):
-                        nc.tensor.matmul_mx(
-                            out=h2T[:, t, :],
-                            lhsT=w_words_sorted[:, g, t, :].bitcast(FP8X4),
-                            lhsT_scale=w_scales_sorted[:, g, t, :],
-                            rhs=g1_codes[(i, s)][:, g, :].bitcast(FP8X4),
-                            rhs_scale=g1_scales[(i, s)][:, g, :],
-                            start=(g == 0),
-                            stop=(g == PASSES - 1),
-                        )
-                g2_grouped[(i, s)] = work.tile([P, P, PACK], BF16, name="g2_grouped", align_bytes=64)
+                    nc.scalar.activation(
+                        out=g2_grouped[i][:, s, :, t],
+                        in_=h2T[(i, s)][:, t, :],
+                        func=mybir.ActivationFunctionType.Identity,
+                        bias=bias_by_code[:, t : t + 1],
+                        scale=1.0,
+                    )
+            else:
                 nc.vector.tensor_tensor(
-                    out=g2_grouped[(i, s)][:],
-                    in0=h2T[:].rearrange("p t c -> p c t"),
+                    out=g2_grouped[i][:, s],
+                    in0=h2T[(i, s)][:].rearrange("p t c -> p c t"),
                     in1=bias_by_code[:].unsqueeze(1).to_broadcast([P, P, PACK]),
                     op=mybir.AluOpType.add,
                 )
 
-        def quantise_g2(i):
-            for s in range(SIDES):
-                g2_codes[(i, s)] = work.tile([P, P], U32, name="g2_codes", align_bytes=64)
-                g2_scales[(i, s)] = work.tile([P, P], U8, name="g2_scales", align_bytes=64)
-                nc.vector.quantize_mx(
-                    out=g2_codes[(i, s)][:].bitcast(FP8X4),
-                    scales=g2_scales[(i, s)][:],
-                    in_=g2_grouped[(i, s)][:].rearrange("p c t -> p (c t)"),
-                )
+        def quantise_g2(i, sides):
+            lo, hi = sides[0], sides[-1] + 1
+            nc.vector.quantize_mx(
+                out=g2_codes[i][:, lo:hi].rearrange("p s c -> p (s c)").bitcast(FP8X4),
+                scales=g2_scales[i][:, lo:hi].rearrange("p s c -> p (s c)"),
+                in_=g2_grouped[i][:, lo:hi].rearrange("p s c t -> p (s c t)"),
+            )
 
         def level_two(i):
+            pieces = LAST_PIECES if i == N_TILES - 1 else 1
+            width = E // pieces
             out_ps = psum.tile([P, E], F32, name="out_ps")
-            for s in range(SIDES):
-                nc.tensor.matmul_mx(
-                    out=out_ps[:],
-                    lhsT=g2_codes[(i, s)][:].bitcast(FP8X4),
-                    lhsT_scale=g2_scales[(i, s)][:],
-                    rhs=w_words[:, s, :].bitcast(FP8X4),
-                    rhs_scale=w_scales[:, s, :],
-                    start=(s == 0),
-                    stop=(s == SIDES - 1),
-                )
             out_sb = work.tile([P, E], F32, name="out_sb")
-            nc.vector.tensor_tensor(
-                out=out_sb[:], in0=out_ps[:], in1=bias_plain[:], op=mybir.AluOpType.add
-            )
-            nc.sync.dma_start(out=out_rows[i * P : (i + 1) * P, :], in_=out_sb[:])
+            for c in range(pieces):
+                cols = slice(c * width, (c + 1) * width)
+                for s in range(SIDES):
+                    nc.tensor.matmul_mx(
+                        out=out_ps[:, cols],
+                        lhsT=g2_codes[i][:, s, :].bitcast(FP8X4),
+                        lhsT_scale=g2_scales[i][:, s, :],
+                        rhs=w_words[:, s, c * width * PACK : (c + 1) * width * PACK].bitcast(FP8X4),
+                        rhs_scale=w_scales[:, s, cols],
+                        start=(s == 0),
+                        stop=(s == SIDES - 1),
+                    )
+            for c in range(pieces):
+                cols = slice(c * width, (c + 1) * width)
+                nc.vector.tensor_tensor(
+                    out=out_sb[:, cols], in0=out_ps[:, cols], in1=bias_plain[:, cols], op=mybir.AluOpType.add
+                )
+                queue = nc.scalar if c % 2 else nc.sync
+                queue.dma_start(out=out_rows[i * P : (i + 1) * P, cols], in_=out_sb[:, cols])
 
         def in_range(i):
             return 0 <= i < N_TILES
 
+        both = list(range(SIDES))
         warm_up()
         spread_bias()
-        for j in range(N_TILES + 2):
-            if in_range(j):
-                quantise_g1(j)
-            if in_range(j - 1):
-                level_one(j - 1)
-                quantise_g2(j - 1)
-            if in_range(j - 2):
-                level_two(j - 2)
+        sort_w_scales()
+        if TILES_BEFORE_W == 0:
+            sort_w_words()
+        for j in range(-LEAD_T, N_TILES + LAG_L2):
+            a, b, c = j + LEAD_T, j, j - LAG_L2
+            if in_range(a):
+                new_g1(a)
+                if a >= SORT_FROM_TILE:
+                    for s in both:
+                        sort_words(a, s)
+                for s in both:
+                    transposes(a, s)
+                    evacuate_x(a, s)
+            if a == TILES_BEFORE_W - 1 or (TILES_BEFORE_W > N_TILES and a == 0):
+                sort_w_words()
+            q1 = [[s] for s in both] if not MERGE_Q1 else [both]
+            q2 = [[s] for s in both] if not MERGE_Q2 else [both]
+            if in_range(b):
+                new_g2(b)
+            if V_ORDER == 0:
+                if in_range(a):
+                    for sides in q1:
+                        quantise_g1(a, sides)
+                if in_range(b):
+                    for s in both:
+                        level_one(b, s)
+                        add_bias(b, s)
+                    for sides in q2:
+                        quantise_g2(b, sides)
+            elif V_ORDER == 1:
+                for s in both:
+                    if in_range(a) and not MERGE_Q1:
+                        quantise_g1(a, [s])
+                    if in_range(a) and MERGE_Q1 and s == 1:
+                        quantise_g1(a, both)
+                    if in_range(b):
+                        level_one(b, s)
+                        add_bias(b, s)
+                if in_range(b):
+                    for sides in q2:
+                        quantise_g2(b, sides)
+            elif V_ORDER == 2:
+                if in_range(b):
+                    for s in both:
+                        level_one(b, s)
+                        add_bias(b, s)
+                if in_range(a):
+                    for sides in q1:
+                        quantise_g1(a, sides)
+                if in_range(b):
+                    for sides in q2:
+                        quantise_g2(b, sides)
+            if in_range(c):
+                level_two(c)

@@ -30,7 +30,7 @@ XT_BANKS = 3
 H2_BANKS = 3
 OUT_BANKS = 2
 SORT_FROM_TILE = 6
-TILES_BEFORE_W = 0
+TILES_BEFORE_W = 1
 LEAD_T = 1
 LAG_L2 = 1
 SCALAR_B = ()

@@ -107,12 +107,12 @@ def tile_simplemodel_pc_kernel(tc, h1, cross_w_words, cross_w_scales, cross_b, o
                     in_=w_words[:, g, :].bitcast(I32).rearrange("p (m t) -> p t m", t=PACK),
                 )
 
-        def warm_up():
+        def warm_up(count):
             unread = psum.tile([P, E], F32, name="h2T", bufs=H2_BANKS)
-            for n in range(WARM_UP_MATMULS):
+            for n in range(count):
                 nc.tensor.matmul(
                     out=unread[:], lhsT=ones[:], rhs=zeros[:],
-                    start=(n == 0), stop=(n == WARM_UP_MATMULS - 1),
+                    start=(n == 0), stop=(n == count - 1),
                 )
 
         bias_plain = keep.tile([P, E], F32)
@@ -238,8 +238,7 @@ def tile_simplemodel_pc_kernel(tc, h1, cross_w_words, cross_w_scales, cross_b, o
             return 0 <= i < N_TILES
 
         both = list(range(SIDES))
-        warm_up()
-        spread_bias()
+        warm_up(WARM_UP_MATMULS)
         sort_w_scales()
         if TILES_BEFORE_W == 0:
             sort_w_words()
@@ -253,7 +252,9 @@ def tile_simplemodel_pc_kernel(tc, h1, cross_w_words, cross_w_scales, cross_b, o
                 for s in both:
                     transposes(a, s)
                     evacuate_x(a, s)
-            if a == TILES_BEFORE_W - 1 or (TILES_BEFORE_W > N_TILES and a == 0):
+            if a == TILES_BEFORE_W - 1:
+                spread_bias()
+                warm_up(3)
                 sort_w_words()
             q1 = [[s] for s in both] if not MERGE_Q1 else [both]
             q2 = [[s] for s in both] if not MERGE_Q2 else [both]

@@ -30,7 +30,6 @@ XT_BANKS = 3
 H2_BANKS = 3
 OUT_BANKS = 2
 SORT_FROM_TILE = 6
-TILES_BEFORE_W = 1
 LEAD_T = 1
 LAG_L2 = 1
 SCALAR_B = ()
@@ -63,33 +62,33 @@ def tile_simplemodel_pc_kernel(tc, h1, cross_w_words, cross_w_scales, cross_b, o
         ident_f32 = keep.tile([P, P], F32)
         make_identity(nc, ident_f32[:])
 
-        nc.scalar.dma_start(out=bias_rows[0:1, :], in_=cross_b.unsqueeze(0))
+        nc.gpsimd.dma_start(out=bias_rows[0:1, :], in_=cross_b.unsqueeze(0))
         bias_by_code = keep.tile([P, PACK], BF16)
-        nc.scalar.dma_start(out=bias_by_code[:], in_=cross_b.rearrange("(p t) -> p t", t=PACK))
+        nc.gpsimd.dma_start(out=bias_by_code[:], in_=cross_b.rearrange("(p t) -> p t", t=PACK))
 
         x_sb = {}
 
-        def load_x(i):
-            for s in range(SIDES):
-                x_sb[(i, s)] = keep.tile([P, K2], BF16, name="x_%d_%d" % (i, s))
-                nc.sync.dma_start(
-                    out=x_sb[(i, s)][:],
-                    in_=x_rows[i * P : (i + 1) * P, s * K2 : (s + 1) * K2],
-                )
+        def load_x(i, sides):
+            if i not in x_sb:
+                x_sb[i] = keep.tile([P, SIDES, K2], BF16, name="x_%d" % i)
+            lo, hi = sides[0], sides[-1] + 1
+            nc.sync.dma_start(
+                out=x_sb[i][:, lo:hi, :].rearrange("p s k -> p (s k)"),
+                in_=x_rows[i * P : (i + 1) * P, lo * K2 : hi * K2],
+            )
 
+        load_x(0, [0])
         scale_words = cross_w_scales.bitcast(I32).rearrange("g (a r) n -> r a g n", r=SCALE_ROWS)
         for r in range(SCALE_ROWS):
             nc.sync.dma_start(out=w_scales[r:P:QUADRANT, :, :].bitcast(I32), in_=scale_words[r])
-        for i in range(TILES_BEFORE_W):
-            load_x(i)
+        load_x(0, [1])
         w_words = keep.tile([P, PASSES, E * PACK], U8, align_bytes=64)
-        for g in range(PASSES):
-            nc.sync.dma_start(
-                out=w_words[:, g, :].bitcast(I32),
-                in_=cross_w_words[g].rearrange("p n t -> p (n t)").bitcast(I32),
-            )
-        for i in range(TILES_BEFORE_W, N_TILES):
-            load_x(i)
+        nc.sync.dma_start(
+            out=w_words[:].rearrange("p g b -> p (g b)").bitcast(I32).rearrange("p (g b) -> p g b", g=PASSES),
+            in_=cross_w_words.rearrange("g p n t -> p g (n t)").bitcast(I32),
+        )
+        for i in range(1, N_TILES):
+            load_x(i, list(range(SIDES)))
 
         w_scales_sorted = keep.tile([P, PASSES, PACK, P], U8, align_bytes=64)
         w_words_sorted = keep.tile([P, PASSES, PACK, P], I32, align_bytes=64)
@@ -129,11 +128,11 @@ def tile_simplemodel_pc_kernel(tc, h1, cross_w_words, cross_w_scales, cross_b, o
             x_sorted[(i, s)] = work.tile([P, PASSES, HALVES, P], F32, name="x_sorted")
             nc.scalar.copy(
                 out=x_sorted[(i, s)][:],
-                in_=x_sb[(i, s)][:].bitcast(F32).rearrange("p (g q u) -> p g u q", g=PASSES, u=HALVES),
+                in_=x_sb[i][:, s, :].bitcast(F32).rearrange("p (g q u) -> p g u q", g=PASSES, u=HALVES),
             )
 
         def transposes(i, s):
-            x_words = x_sb[(i, s)][:].bitcast(F32)
+            x_words = x_sb[i][:, s, :].bitcast(F32)
             xT[(i, s)] = psum.tile([P, PASSES, HALVES, P], F32, name="xT", bufs=XT_BANKS)
             for g in range(PASSES):
                 for u in range(HALVES):
@@ -240,8 +239,6 @@ def tile_simplemodel_pc_kernel(tc, h1, cross_w_words, cross_w_scales, cross_b, o
         both = list(range(SIDES))
         warm_up(WARM_UP_MATMULS)
         sort_w_scales()
-        if TILES_BEFORE_W == 0:
-            sort_w_words()
         for j in range(-LEAD_T, N_TILES + LAG_L2):
             a, b, c = j + LEAD_T, j, j - LAG_L2
             if in_range(a):
@@ -252,7 +249,7 @@ def tile_simplemodel_pc_kernel(tc, h1, cross_w_words, cross_w_scales, cross_b, o
                 for s in both:
                     transposes(a, s)
                     evacuate_x(a, s)
-            if a == TILES_BEFORE_W - 1:
+            if a == 0:
                 spread_bias()
                 warm_up(3)
                 sort_w_words()

@@ -53,8 +53,6 @@ def tile_simplemodel_pc_kernel(tc, h1, cross_w_words, cross_w_scales, cross_b, o
 
         w_scales = keep.tile([P, PASSES, E], U8, align_bytes=64)
         nc.gpsimd.memset(w_scales[:].bitcast(F32), 0.0)
-        bias_rows = keep.tile([P, E], BF16)
-        nc.vector.memset(bias_rows[:], 0.0)
         ones = keep.tile([P, P], BF16)
         nc.vector.memset(ones[:], 1.0)
         zeros = keep.tile([P, E], BF16)
@@ -62,9 +60,9 @@ def tile_simplemodel_pc_kernel(tc, h1, cross_w_words, cross_w_scales, cross_b, o
         ident_f32 = keep.tile([P, P], F32)
         make_identity(nc, ident_f32[:])
 
-        nc.gpsimd.dma_start(out=bias_rows[0:1, :], in_=cross_b.unsqueeze(0))
         bias_by_code = keep.tile([P, PACK], BF16)
-        nc.gpsimd.dma_start(out=bias_by_code[:], in_=cross_b.rearrange("(p t) -> p t", t=PACK))
+        nc.scalar.dma_start(out=bias_by_code[:], in_=cross_b.rearrange("(p t) -> p t", t=PACK))
+        bias_rows = keep.tile([P, P, PACK], BF16)
 
         x_sb = {}
 
@@ -116,9 +114,17 @@ def tile_simplemodel_pc_kernel(tc, h1, cross_w_words, cross_w_scales, cross_b, o
 
         bias_plain = keep.tile([P, E], F32)
 
+        def lay_bias_rows():
+            nc.vector.tensor_tensor(
+                out=bias_rows[:],
+                in0=ident_f32[:].unsqueeze(2).to_broadcast([P, P, PACK]),
+                in1=bias_by_code[:].unsqueeze(1).to_broadcast([P, P, PACK]),
+                op=mybir.AluOpType.mult,
+            )
+
         def spread_bias():
             bias_ps = psum.tile([P, E], F32, name="out_ps")
-            nc.tensor.matmul(out=bias_ps[:], lhsT=ones[:], rhs=bias_rows[:], start=True, stop=True)
+            nc.tensor.matmul(out=bias_ps[:], lhsT=ones[:], rhs=bias_rows[:].rearrange("p m t -> p (m t)"), start=True, stop=True)
             nc.scalar.copy(out=bias_plain[:], in_=bias_ps[:])
 
         x_sorted, xT, g1_grouped, g1_codes, g1_scales = {}, {}, {}, {}, {}
@@ -239,6 +245,7 @@ def tile_simplemodel_pc_kernel(tc, h1, cross_w_words, cross_w_scales, cross_b, o
         both = list(range(SIDES))
         warm_up(WARM_UP_MATMULS)
         sort_w_scales()
+        lay_bias_rows()
         for j in range(-LEAD_T, N_TILES + LAG_L2):
             a, b, c = j + LEAD_T, j, j - LAG_L2
             if in_range(a):

@@ -32,10 +32,10 @@ OUT_BANKS = 2
 SORT_FROM_TILE = 6
 LEAD_T = 1
 LAG_L2 = 1
-SCALAR_B = ()
+SCALAR_B = ((3, 0), (5, 0))
 MERGE_Q1 = False
 MERGE_Q2 = False
-V_ORDER = 0
+V_ORDER = 1
 LAST_PIECES = 2
 WARM_UP_MATMULS = 5
 

@@ -31,11 +31,8 @@ H2_BANKS = 3
 OUT_BANKS = 2
 SORT_FROM_TILE = 6
 LEAD_T = 1
-LAG_L2 = 1
+LAG_L2 = 2
 SCALAR_B = ((3, 0), (5, 0))
-MERGE_Q1 = False
-MERGE_Q2 = False
-V_ORDER = 1
 LAST_PIECES = 2
 WARM_UP_MATMULS = 5
 
@@ -85,7 +82,9 @@ def tile_simplemodel_pc_kernel(tc, h1, cross_w_words, cross_w_scales, cross_b, o
             out=w_words[:].rearrange("p g b -> p (g b)").bitcast(I32).rearrange("p (g b) -> p g b", g=PASSES),
             in_=cross_w_words.rearrange("g p n t -> p g (n t)").bitcast(I32),
         )
-        for i in range(1, N_TILES):
+        for s in range(SIDES):
+            load_x(1, [s])
+        for i in range(2, N_TILES):
             load_x(i, list(range(SIDES)))
 
         w_scales_sorted = keep.tile([P, PASSES, PACK, P], U8, align_bytes=64)
@@ -260,42 +259,16 @@ def tile_simplemodel_pc_kernel(tc, h1, cross_w_words, cross_w_scales, cross_b, o
                 spread_bias()
                 warm_up(3)
                 sort_w_words()
-            q1 = [[s] for s in both] if not MERGE_Q1 else [both]
-            q2 = [[s] for s in both] if not MERGE_Q2 else [both]
             if in_range(b):
                 new_g2(b)
-            if V_ORDER == 0:
+            for s in both:
                 if in_range(a):
-                    for sides in q1:
-                        quantise_g1(a, sides)
+                    quantise_g1(a, [s])
                 if in_range(b):
-                    for s in both:
-                        level_one(b, s)
-                        add_bias(b, s)
-                    for sides in q2:
-                        quantise_g2(b, sides)
-            elif V_ORDER == 1:
-                for s in both:
-                    if in_range(a) and not MERGE_Q1:
-                        quantise_g1(a, [s])
-                    if in_range(a) and MERGE_Q1 and s == 1:
-                        quantise_g1(a, both)
-                    if in_range(b):
-                        level_one(b, s)
-                        add_bias(b, s)
-                if in_range(b):
-                    for sides in q2:
-                        quantise_g2(b, sides)
-            elif V_ORDER == 2:
-                if in_range(b):
-                    for s in both:
-                        level_one(b, s)
-                        add_bias(b, s)
-                if in_range(a):
-                    for sides in q1:
-                        quantise_g1(a, sides)
-                if in_range(b):
-                    for sides in q2:
-                        quantise_g2(b, sides)
+                    level_one(b, s)
+                    add_bias(b, s)
             if in_range(c):
                 level_two(c)
+            if in_range(b):
+                for s in both:
+                    quantise_g2(b, [s])

@@ -58,9 +58,9 @@ def tile_simplemodel_pc_kernel(tc, h1, cross_w_words, cross_w_scales, cross_b, o
         make_identity(nc, ident_f32[:])
 
         bias_by_code = keep.tile([P, PACK], BF16)
-        nc.scalar.dma_start(out=bias_by_code[:], in_=cross_b.rearrange("(p t) -> p t", t=PACK))
-        bias_rows = keep.tile([P, P, PACK], BF16)
+        bias_plain = keep.tile([P, E], BF16)
 
+        both = list(range(SIDES))
         x_sb = {}
 
         def load_x(i, sides):
@@ -72,20 +72,21 @@ def tile_simplemodel_pc_kernel(tc, h1, cross_w_words, cross_w_scales, cross_b, o
                 in_=x_rows[i * P : (i + 1) * P, lo * K2 : hi * K2],
             )
 
-        load_x(0, [0])
+        load_x(0, both)
         scale_words = cross_w_scales.bitcast(I32).rearrange("g (a r) n -> r a g n", r=SCALE_ROWS)
         for r in range(SCALE_ROWS):
             nc.sync.dma_start(out=w_scales[r:P:QUADRANT, :, :].bitcast(I32), in_=scale_words[r])
-        load_x(0, [1])
         w_words = keep.tile([P, PASSES, E * PACK], U8, align_bytes=64)
         nc.sync.dma_start(
             out=w_words[:].rearrange("p g b -> p (g b)").bitcast(I32).rearrange("p (g b) -> p g b", g=PASSES),
             in_=cross_w_words.rearrange("g p n t -> p g (n t)").bitcast(I32),
         )
-        for s in range(SIDES):
+        for s in both:
             load_x(1, [s])
+        nc.sync.dma_start(out=bias_by_code[:], in_=cross_b.rearrange("(p t) -> p t", t=PACK))
         for i in range(2, N_TILES):
-            load_x(i, list(range(SIDES)))
+            load_x(i, both)
+        nc.sync.dma_start(out=bias_plain[:], in_=cross_b.partition_broadcast(P))
 
         w_scales_sorted = keep.tile([P, PASSES, PACK, P], U8, align_bytes=64)
         w_words_sorted = keep.tile([P, PASSES, PACK, P], I32, align_bytes=64)
@@ -99,8 +100,8 @@ def tile_simplemodel_pc_kernel(tc, h1, cross_w_words, cross_w_scales, cross_b, o
         def sort_w_words():
             for g in range(PASSES):
                 nc.vector.tensor_copy(
-                    out=w_words_sorted[:, g, :, :],
-                    in_=w_words[:, g, :].bitcast(I32).rearrange("p (m t) -> p t m", t=PACK),
+                    out=w_words_sorted[:, g, :, :].rearrange("p t m -> p m t"),
+                    in_=w_words[:, g, :].bitcast(I32).rearrange("p (m t) -> p m t", t=PACK),
                 )
 
         def warm_up(count):
@@ -110,21 +111,6 @@ def tile_simplemodel_pc_kernel(tc, h1, cross_w_words, cross_w_scales, cross_b, o
                     out=unread[:], lhsT=ones[:], rhs=zeros[:],
                     start=(n == 0), stop=(n == count - 1),
                 )
-
-        bias_plain = keep.tile([P, E], F32)
-
-        def lay_bias_rows():
-            nc.vector.tensor_tensor(
-                out=bias_rows[:],
-                in0=ident_f32[:].unsqueeze(2).to_broadcast([P, P, PACK]),
-                in1=bias_by_code[:].unsqueeze(1).to_broadcast([P, P, PACK]),
-                op=mybir.AluOpType.mult,
-            )
-
-        def spread_bias():
-            bias_ps = psum.tile([P, E], F32, name="out_ps")
-            nc.tensor.matmul(out=bias_ps[:], lhsT=ones[:], rhs=bias_rows[:].rearrange("p m t -> p (m t)"), start=True, stop=True)
-            nc.scalar.copy(out=bias_plain[:], in_=bias_ps[:])
 
         x_sorted, xT, g1_grouped, g1_codes, g1_scales = {}, {}, {}, {}, {}
         h2T, g2_grouped, g2_codes, g2_scales = {}, {}, {}, {}
@@ -241,10 +227,8 @@ def tile_simplemodel_pc_kernel(tc, h1, cross_w_words, cross_w_scales, cross_b, o
         def in_range(i):
             return 0 <= i < N_TILES
 
-        both = list(range(SIDES))
         warm_up(WARM_UP_MATMULS)
         sort_w_scales()
-        lay_bias_rows()
         for j in range(-LEAD_T, N_TILES + LAG_L2):
             a, b, c = j + LEAD_T, j, j - LAG_L2
             if in_range(a):
@@ -256,7 +240,6 @@ def tile_simplemodel_pc_kernel(tc, h1, cross_w_words, cross_w_scales, cross_b, o
                     transposes(a, s)
                     evacuate_x(a, s)
             if a == 0:
-                spread_bias()
                 warm_up(3)
                 sort_w_words()
             if in_range(b):

from contextlib import ExitStack

import concourse.mybir as mybir
from concourse.masks import make_identity

BF16 = mybir.dt.bfloat16
F32 = mybir.dt.float32
I32 = mybir.dt.int32
U32 = mybir.dt.uint32
U8 = mybir.dt.uint8
FP8X4 = mybir.dt.float8_e4m3fn_x4

P = 128
PACK = 4
K_PASS = P * PACK
E = 512
K2 = 2 * E
PASSES = K2 // K_PASS
SIDES = 2
HALVES = 2
ROWS_OUT = 24 * 16 * 2
N_TILES = ROWS_OUT // P
SCALE_ROWS = 4
QUADRANT = 32

FLOPS = 2 * (SIDES * ROWS_OUT) * K2 * E + 2 * ROWS_OUT * K2 * E

WORK_BUFS = 2 * SIDES
XT_BANKS = 3
H2_BANKS = 3
OUT_BANKS = 2
SORT_FROM_TILE = 6
LEAD_T = 1
LAG_L2 = 2
SCALAR_B = ((3, 0), (5, 0))
LAST_PIECES = 2
WARM_UP_MATMULS = 5


def tile_simplemodel_pc_kernel(tc, h1, cross_w_words, cross_w_scales, cross_b, out):
    nc = tc.nc
    x_rows = h1.flatten_outer_dims().rearrange("(r c) k -> r (c k)", c=SIDES * 2)
    out_rows = out.flatten_outer_dims()

    with ExitStack() as stack:
        keep = stack.enter_context(tc.tile_pool(name="keep", bufs=1))
        work = stack.enter_context(tc.tile_pool(name="work", bufs=WORK_BUFS))
        psum = stack.enter_context(tc.psum_pool(name="psum", bufs=OUT_BANKS))
        stack.enter_context(tc.manual_schedule())

        w_scales = keep.tile([P, PASSES, E], U8, align_bytes=64)
        nc.gpsimd.memset(w_scales[:].bitcast(F32), 0.0)
        ones = keep.tile([P, P], BF16)
        nc.vector.memset(ones[:], 1.0)
        zeros = keep.tile([P, E], BF16)
        nc.vector.memset(zeros[:], 0.0)
        ident_f32 = keep.tile([P, P], F32)
        make_identity(nc, ident_f32[:])

        bias_by_code = keep.tile([P, PACK], BF16)
        bias_plain = keep.tile([P, E], BF16)

        both = list(range(SIDES))
        x_sb = {}

        def load_x(i, sides):
            if i not in x_sb:
                x_sb[i] = keep.tile([P, SIDES, K2], BF16, name="x_%d" % i)
            lo, hi = sides[0], sides[-1] + 1
            nc.sync.dma_start(
                out=x_sb[i][:, lo:hi, :].rearrange("p s k -> p (s k)"),
                in_=x_rows[i * P : (i + 1) * P, lo * K2 : hi * K2],
            )

        load_x(0, both)
        scale_words = cross_w_scales.bitcast(I32).rearrange("g (a r) n -> r a g n", r=SCALE_ROWS)
        for r in range(SCALE_ROWS):
            nc.sync.dma_start(out=w_scales[r:P:QUADRANT, :, :].bitcast(I32), in_=scale_words[r])
        w_words = keep.tile([P, PASSES, E * PACK], U8, align_bytes=64)
        nc.sync.dma_start(
            out=w_words[:].rearrange("p g b -> p (g b)").bitcast(I32).rearrange("p (g b) -> p g b", g=PASSES),
            in_=cross_w_words.rearrange("g p n t -> p g (n t)").bitcast(I32),
        )
        for s in both:
            load_x(1, [s])
        nc.sync.dma_start(out=bias_by_code[:], in_=cross_b.rearrange("(p t) -> p t", t=PACK))
        for i in range(2, N_TILES):
            load_x(i, both)
        nc.sync.dma_start(out=bias_plain[:], in_=cross_b.partition_broadcast(P))

        w_scales_sorted = keep.tile([P, PASSES, PACK, P], U8, align_bytes=64)
        w_words_sorted = keep.tile([P, PASSES, PACK, P], I32, align_bytes=64)

        def sort_w_scales():
            nc.vector.tensor_copy(
                out=w_scales_sorted[:].rearrange("p g t m -> p g m t"),
                in_=w_scales[:].rearrange("p g (m t) -> p g m t", t=PACK),
            )

        def sort_w_words():
            for g in range(PASSES):
                nc.vector.tensor_copy(
                    out=w_words_sorted[:, g, :, :].rearrange("p t m -> p m t"),
                    in_=w_words[:, g, :].bitcast(I32).rearrange("p (m t) -> p m t", t=PACK),
                )

        def warm_up(count):
            unread = psum.tile([P, E], F32, name="h2T", bufs=H2_BANKS)
            for n in range(count):
                nc.tensor.matmul(
                    out=unread[:], lhsT=ones[:], rhs=zeros[:],
                    start=(n == 0), stop=(n == count - 1),
                )

        x_sorted, xT, g1_grouped, g1_codes, g1_scales = {}, {}, {}, {}, {}
        h2T, g2_grouped, g2_codes, g2_scales = {}, {}, {}, {}

        def sort_words(i, s):
            x_sorted[(i, s)] = work.tile([P, PASSES, HALVES, P], F32, name="x_sorted")
            nc.scalar.copy(
                out=x_sorted[(i, s)][:],
                in_=x_sb[i][:, s, :].bitcast(F32).rearrange("p (g q u) -> p g u q", g=PASSES, u=HALVES),
            )

        def transposes(i, s):
            x_words = x_sb[i][:, s, :].bitcast(F32)
            xT[(i, s)] = psum.tile([P, PASSES, HALVES, P], F32, name="xT", bufs=XT_BANKS)
            for g in range(PASSES):
                for u in range(HALVES):
                    first = g * (K_PASS // 2) + u
                    nc.tensor.transpose(
                        xT[(i, s)][:, g, u, :],
                        x_sorted[(i, s)][:, g, u, :]
                        if i >= SORT_FROM_TILE
                        else x_words[:, first : (g + 1) * (K_PASS // 2) : HALVES],
                        ident_f32[:],
                    )

        def new_g1(i):
            g1_grouped[i] = work.tile([P, SIDES, PASSES, P, PACK], BF16, name="g1_grouped", bufs=SIDES, align_bytes=64)
            g1_codes[i] = work.tile([P, SIDES, PASSES, P], U32, name="g1_codes", bufs=3, align_bytes=64)
            g1_scales[i] = work.tile([P, SIDES, PASSES, P], U8, name="g1_scales", bufs=3, align_bytes=64)

        def evacuate_x(i, s):
            nc.scalar.copy(
                out=g1_grouped[i][:, s].bitcast(F32), in_=xT[(i, s)][:].rearrange("p g u c -> p g c u")
            )

        def quantise_g1(i, sides):
            lo, hi = sides[0], sides[-1] + 1
            nc.vector.quantize_mx(
                out=g1_codes[i][:, lo:hi].rearrange("p s g c -> p (s g c)").bitcast(FP8X4),
                scales=g1_scales[i][:, lo:hi].rearrange("p s g c -> p (s g c)"),
                in_=g1_grouped[i][:, lo:hi].rearrange("p s g c t -> p (s g c t)"),
            )

        def level_one(i, s):
            h2T[(i, s)] = psum.tile([P, PACK, P], F32, name="h2T", bufs=H2_BANKS)
            for t in range(PACK):
                for g in range(PASSES):
                    nc.tensor.matmul_mx(
                        out=h2T[(i, s)][:, t, :],
                        lhsT=w_words_sorted[:, g, t, :].bitcast(FP8X4),
                        lhsT_scale=w_scales_sorted[:, g, t, :],
                        rhs=g1_codes[i][:, s, g, :].bitcast(FP8X4),
                        rhs_scale=g1_scales[i][:, s, g, :],
                        start=(g == 0),
                        stop=(g == PASSES - 1),
                    )

        def new_g2(i):
            g2_grouped[i] = work.tile([P, SIDES, P, PACK], BF16, name="g2_grouped", bufs=3, align_bytes=64)
            g2_codes[i] = work.tile([P, SIDES, P], U32, name="g2_codes", bufs=3, align_bytes=64)
            g2_scales[i] = work.tile([P, SIDES, P], U8, name="g2_scales", bufs=3, align_bytes=64)

        def add_bias(i, s):
            if (i, s) in SCALAR_B:
                for t in range(PACK):
                    nc.scalar.activation(
                        out=g2_grouped[i][:, s, :, t],
                        in_=h2T[(i, s)][:, t, :],
                        func=mybir.ActivationFunctionType.Identity,
                        bias=bias_by_code[:, t : t + 1],
                        scale=1.0,
                    )
            else:
                nc.vector.tensor_tensor(
                    out=g2_grouped[i][:, s],
                    in0=h2T[(i, s)][:].rearrange("p t c -> p c t"),
                    in1=bias_by_code[:].unsqueeze(1).to_broadcast([P, P, PACK]),
                    op=mybir.AluOpType.add,
                )

        def quantise_g2(i, sides):
            lo, hi = sides[0], sides[-1] + 1
            nc.vector.quantize_mx(
                out=g2_codes[i][:, lo:hi].rearrange("p s c -> p (s c)").bitcast(FP8X4),
                scales=g2_scales[i][:, lo:hi].rearrange("p s c -> p (s c)"),
                in_=g2_grouped[i][:, lo:hi].rearrange("p s c t -> p (s c t)"),
            )

        def level_two(i):
            pieces = LAST_PIECES if i == N_TILES - 1 else 1
            width = E // pieces
            out_ps = psum.tile([P, E], F32, name="out_ps")
            out_sb = work.tile([P, E], F32, name="out_sb")
            for c in range(pieces):
                cols = slice(c * width, (c + 1) * width)
                for s in range(SIDES):
                    nc.tensor.matmul_mx(
                        out=out_ps[:, cols],
                        lhsT=g2_codes[i][:, s, :].bitcast(FP8X4),
                        lhsT_scale=g2_scales[i][:, s, :],
                        rhs=w_words[:, s, c * width * PACK : (c + 1) * width * PACK].bitcast(FP8X4),
                        rhs_scale=w_scales[:, s, cols],
                        start=(s == 0),
                        stop=(s == SIDES - 1),
                    )
            for c in range(pieces):
                cols = slice(c * width, (c + 1) * width)
                nc.vector.tensor_tensor(
                    out=out_sb[:, cols], in0=out_ps[:, cols], in1=bias_plain[:, cols], op=mybir.AluOpType.add
                )
                queue = nc.scalar if c % 2 else nc.sync
                queue.dma_start(out=out_rows[i * P : (i + 1) * P, cols], in_=out_sb[:, cols])

        def in_range(i):
            return 0 <= i < N_TILES

        warm_up(WARM_UP_MATMULS)
        sort_w_scales()
        for j in range(-LEAD_T, N_TILES + LAG_L2):
            a, b, c = j + LEAD_T, j, j - LAG_L2
            if in_range(a):
                new_g1(a)
                if a >= SORT_FROM_TILE:
                    for s in both:
                        sort_words(a, s)
                for s in both:
                    transposes(a, s)
                    evacuate_x(a, s)
            if a == 0:
                warm_up(3)
                sort_w_words()
            if in_range(b):
                new_g2(b)
            for s in both:
                if in_range(a):
                    quantise_g1(a, [s])
                if in_range(b):
                    level_one(b, s)
                    add_bias(b, s)
            if in_range(c):
                level_two(c)
            if in_range(b):
                for s in both:
                    quantise_g2(b, [s])
